import numpy as np
import ml_dtypes

BF16 = ml_dtypes.bfloat16


def bf(x):
    return np.asarray(x, np.float32).astype(BF16)


def f32(x):
    return np.asarray(x, np.float32)


def f64(x):
    return np.asarray(x).astype(np.float64)


def striped(idx):
    return np.tile(idx.reshape(-1, 16).T, (8, 1))


C, H, S, N = 256, 1024, 4096, 2048
EPS = 1e-5


def setup_inputs():
    base = f32(np.random.standard_normal((C, S)))
    x = f32(np.random.standard_normal((C, N)) * (0.5 + np.random.random((1, N))) + 0.5 * np.random.standard_normal((1, N)))
    ln_w = f32(1.0 + 0.1 * np.random.standard_normal((C, 1)))
    ln_b = f32(0.1 * np.random.standard_normal((C, 1)))
    wck = bf(np.random.standard_normal((C, H)) / np.sqrt(C))
    wcv = bf(np.random.standard_normal((H, C)) / np.sqrt(H))
    return {"base": base, "x": x, "ln_w": ln_w, "ln_b": ln_b, "wck": wck, "wcv": wcv, "offs": striped(np.random.permutation(S)[:N])}


def reference(base, x, ln_w, ln_b, wck, wcv, offs):
    idx = offs[:16].T.reshape(-1)
    xs = f64(x)
    mu = xs.mean(axis=0, keepdims=True)
    var = np.square(xs - mu).mean(axis=0, keepdims=True)
    xn = (xs - mu) / np.sqrt(var + EPS) * f64(ln_w) + f64(ln_b)
    hid = np.square(np.maximum(f64(wck).T @ xn, 0.0))
    y = f64(wcv).T @ hid
    res = f64(base).copy()
    res[:, idx] = xs + y
    return res

@@ -1,0 +1,132 @@
+import concourse.mybir as mybir
+
+F32 = mybir.dt.float32
+BF16 = mybir.dt.bfloat16
+U16 = mybir.dt.uint16
+ALU = mybir.AluOpType
+ACT = mybir.ActivationFunctionType
+
+P = 128
+C = 256
+H = 1024
+S = 4096
+N = 2048
+CB = C // P
+HB = H // P
+T = 512
+NT = N // T
+EPS = 1e-5
+
+FLOPS = 2 * 2 * C * H * N
+
+
+def tile_rwkv8_rosa_block_kernel(tc, base, x, ln_w, ln_b, wck, wcv, offs, out):
+    nc = tc.nc
+    with (
+        tc.tile_pool(name="held", bufs=1) as held,
+        tc.tile_pool(name="norm", bufs=2) as norm,
+        tc.tile_pool(name="relu", bufs=4) as relu,
+        tc.psum_pool(name="stat_ps", bufs=1) as stat_ps,
+        tc.psum_pool(name="h_ps", bufs=4) as h_ps,
+        tc.psum_pool(name="y_ps", bufs=2) as y_ps,
+    ):
+        offsets = held.tile([P, N // 16], U16, name="offsets")
+        x_sb = [held.tile([P, N], F32, name=f"x{b}") for b in range(CB)]
+        window = [held.tile([P, S], F32, name=f"window{b}") for b in range(CB)]
+        y_sb = [held.tile([P, N], F32, name=f"y{b}") for b in range(CB)]
+        xn = held.tile([P, CB, N], BF16, name="xn")
+        hid = held.tile([P, HB, N], BF16, name="hid")
+        wck_sb = held.tile([P, CB, H], BF16, name="wck_sb")
+        wcv_sb = held.tile([P, HB, C], BF16, name="wcv_sb")
+        gain = held.tile([P, CB], F32, name="gain")
+        bias = held.tile([P, CB], F32, name="bias")
+        eps = held.tile([P, 1], F32, name="eps")
+        avg_f32 = held.tile([P, P], F32, name="avg_f32")
+        avg_bf16 = held.tile([P, P], BF16, name="avg_bf16")
+
+        for t in range(NT):
+            for b in range(CB):
+                nc.sync.dma_start(
+                    x_sb[b][:, t * T : (t + 1) * T],
+                    x[b * P : (b + 1) * P, t * T : (t + 1) * T],
+                )
+        nc.sync.dma_start(offsets[:], offs)
+        for b in range(CB):
+            nc.sync.dma_start(window[b][:], base[b * P : (b + 1) * P, :])
+        nc.scalar.dma_start(wck_sb[:], wck.rearrange("(b p) h -> p b h", p=P))
+        nc.scalar.dma_start(wcv_sb[:], wcv.rearrange("(b p) c -> p b c", p=P))
+        with nc.allow_non_contiguous_dma(reason="one gain and one bias to a partition"):
+            nc.gpsimd.dma_start(gain[:], ln_w.rearrange("(b p) o -> p (b o)", p=P))
+            nc.gpsimd.dma_start(bias[:], ln_b.rearrange("(b p) o -> p (b o)", p=P))
+
+        nc.vector.memset(avg_f32[:], 1.0 / C)
+        nc.vector.memset(avg_bf16[:], 1.0 / C)
+        nc.vector.memset(eps[:], EPS)
+
+        def layer_norm(t):
+            tok = slice(t * T, (t + 1) * T)
+            pair = norm.tile([P, T], F32, name="pair")
+            nc.gpsimd.tensor_tensor(pair[:], x_sb[0][:, tok], x_sb[1][:, tok], ALU.add)
+            mean = stat_ps.tile([P, T], F32, name="mean")
+            nc.tensor.matmul(mean[:], avg_f32[:], pair[:], start=True, stop=True)
+            xc = norm.tile([P, CB, T], F32, name="xc")
+            sq = norm.tile([P, CB, T], BF16, name="sq")
+            var = stat_ps.tile([P, T], F32, name="var")
+            for b in range(CB):
+                nc.vector.tensor_tensor(xc[:, b, :], x_sb[b][:, tok], mean[:], ALU.subtract)
+                nc.gpsimd.tensor_tensor(sq[:, b, :], xc[:, b, :], xc[:, b, :], ALU.mult)
+                nc.tensor.matmul(
+                    var[:], avg_bf16[:], sq[:, b, :], start=(b == 0), stop=(b == CB - 1)
+                )
+            std = norm.tile([P, T], F32, name="std")
+            nc.scalar.activation(std[:], var[:], ACT.Sqrt, bias=eps[:])
+            rstd = norm.tile([P, T], F32, name="rstd")
+            nc.vector.reciprocal(rstd[:], std[:])
+            xhat = norm.tile([P, CB, T], F32, name="xhat")
+            for b in range(CB):
+                nc.vector.tensor_tensor(xhat[:, b, :], xc[:, b, :], rstd[:], ALU.mult)
+                nc.gpsimd.tensor_scalar(
+                    xn[:, b, tok], xhat[:, b, :], gain[:, b : b + 1], bias[:, b : b + 1],
+                    ALU.mult, ALU.add,
+                )
+
+        def hidden(t):
+            tok = slice(t * T, (t + 1) * T)
+            for hb in range(HB):
+                h = h_ps.tile([P, T], F32, name="h")
+                for b in range(CB):
+                    nc.tensor.matmul(
+                        h[:], wck_sb[:, b, hb * P : (hb + 1) * P], xn[:, b, tok],
+                        start=(b == 0), stop=(b == CB - 1),
+                    )
+                r = relu.tile([P, T], F32, name="r")
+                nc.scalar.activation(r[:], h[:], ACT.Relu)
+                nc.vector.tensor_tensor(hid[:, hb, tok], r[:], r[:], ALU.mult)
+
+        def project(b, t):
+            tok = slice(t * T, (t + 1) * T)
+            y = y_ps.tile([P, T], F32, name="y")
+            for hb in range(HB):
+                nc.tensor.matmul(
+                    y[:], wcv_sb[:, hb, b * P : (b + 1) * P], hid[:, hb, tok],
+                    start=(hb == 0), stop=(hb == HB - 1),
+                )
+            nc.scalar.copy(y_sb[b][:, tok], y[:])
+
+        def place(b):
+            nc.vector.tensor_tensor(
+                window[b][:].indirect(offsets[:]), x_sb[b][:], y_sb[b][:], ALU.add
+            )
+            nc.sync.dma_start(out[b * P : (b + 1) * P, :], window[b][:])
+
+        layer_norm(0)
+        layer_norm(1)
+        for t in range(NT):
+            hidden(t)
+            if t + 2 < NT:
+                layer_norm(t + 2)
+            project(0, t)
+        place(0)
+        for t in range(NT):
+            project(1, t)
+        place(1)

@@ -78,10 +78,8 @@ def tile_rwkv8_rosa_block_kernel(tc, base, x, ln_w, ln_b, wck, wcv, offs, out):
                 nc.tensor.matmul(
                     var[:], avg_bf16[:], sq[:, b, :], start=(b == 0), stop=(b == CB - 1)
                 )
-            std = norm.tile([P, T], F32, name="std")
-            nc.scalar.activation(std[:], var[:], ACT.Sqrt, bias=eps[:])
             rstd = norm.tile([P, T], F32, name="rstd")
-            nc.vector.reciprocal(rstd[:], std[:])
+            nc.scalar.activation(rstd[:], var[:], ACT.Abs_reciprocal_sqrt, bias=eps[:])
             xhat = norm.tile([P, CB, T], F32, name="xhat")
             for b in range(CB):
                 nc.vector.tensor_tensor(xhat[:, b, :], xc[:, b, :], rstd[:], ALU.mult)

@@ -14,7 +14,9 @@ N = 2048
 CB = C // P
 HB = H // P
 T = 512
-NT = N // T
+WIDTHS = (T // 2, T // 2, T, T, T)
+NT = len(WIDTHS)
+assert sum(WIDTHS) == N
 EPS = 1e-5
 
 FLOPS = 2 * 2 * C * H * N
@@ -24,10 +26,11 @@ def tile_rwkv8_rosa_block_kernel(tc, base, x, ln_w, ln_b, wck, wcv, offs, out):
     nc = tc.nc
     with (
         tc.tile_pool(name="held", bufs=1) as held,
-        tc.tile_pool(name="norm", bufs=2) as norm,
-        tc.tile_pool(name="relu", bufs=4) as relu,
-        tc.psum_pool(name="stat_ps", bufs=1) as stat_ps,
-        tc.psum_pool(name="h_ps", bufs=4) as h_ps,
+        tc.tile_pool(name="norm", bufs=3) as norm,
+        tc.tile_pool(name="relu", bufs=6) as relu,
+        tc.psum_pool(name="mean_ps", bufs=2) as mean_ps,
+        tc.psum_pool(name="var_ps", bufs=1) as var_ps,
+        tc.psum_pool(name="h_ps", bufs=3) as h_ps,
         tc.psum_pool(name="y_ps", bufs=2) as y_ps,
     ):
         offsets = held.tile([P, N // 16], U16, name="offsets")
@@ -44,66 +47,65 @@ def tile_rwkv8_rosa_block_kernel(tc, base, x, ln_w, ln_b, wck, wcv, offs, out):
         avg_f32 = held.tile([P, P], F32, name="avg_f32")
         avg_bf16 = held.tile([P, P], BF16, name="avg_bf16")
 
+        chunk = [slice(sum(WIDTHS[:t]), sum(WIDTHS[: t + 1])) for t in range(NT)]
+
         for t in range(NT):
             for b in range(CB):
-                nc.sync.dma_start(
-                    x_sb[b][:, t * T : (t + 1) * T],
-                    x[b * P : (b + 1) * P, t * T : (t + 1) * T],
-                )
+                nc.sync.dma_start(x_sb[b][:, chunk[t]], x[b * P : (b + 1) * P, chunk[t]])
         nc.sync.dma_start(offsets[:], offs)
         for b in range(CB):
             nc.sync.dma_start(window[b][:], base[b * P : (b + 1) * P, :])
+        with nc.allow_non_contiguous_dma(reason="one gain and one bias to a partition"):
+            nc.scalar.dma_start(gain[:], ln_w.rearrange("(b p) o -> p (b o)", p=P))
+            nc.scalar.dma_start(bias[:], ln_b.rearrange("(b p) o -> p (b o)", p=P))
         nc.scalar.dma_start(wck_sb[:], wck.rearrange("(b p) h -> p b h", p=P))
         nc.scalar.dma_start(wcv_sb[:], wcv.rearrange("(b p) c -> p b c", p=P))
-        with nc.allow_non_contiguous_dma(reason="one gain and one bias to a partition"):
-            nc.gpsimd.dma_start(gain[:], ln_w.rearrange("(b p) o -> p (b o)", p=P))
-            nc.gpsimd.dma_start(bias[:], ln_b.rearrange("(b p) o -> p (b o)", p=P))
 
         nc.vector.memset(avg_f32[:], 1.0 / C)
         nc.vector.memset(avg_bf16[:], 1.0 / C)
         nc.vector.memset(eps[:], EPS)
 
         def layer_norm(t):
-            tok = slice(t * T, (t + 1) * T)
-            pair = norm.tile([P, T], F32, name="pair")
-            nc.gpsimd.tensor_tensor(pair[:], x_sb[0][:, tok], x_sb[1][:, tok], ALU.add)
-            mean = stat_ps.tile([P, T], F32, name="mean")
+            tok, w = chunk[t], WIDTHS[t]
+            pair = norm.tile([P, w], F32, name="pair")
+            nc.vector.tensor_tensor(pair[:], x_sb[0][:, tok], x_sb[1][:, tok], ALU.add)
+            mean = mean_ps.tile([P, w], F32, name="mean")
             nc.tensor.matmul(mean[:], avg_f32[:], pair[:], start=True, stop=True)
-            xc = norm.tile([P, CB, T], F32, name="xc")
-            sq = norm.tile([P, CB, T], BF16, name="sq")
-            var = stat_ps.tile([P, T], F32, name="var")
+            xc = norm.tile([P, CB, w], F32, name="xc")
+            sq = norm.tile([P, CB, w], BF16, name="sq")
+            var = var_ps.tile([P, w], F32, name="var")
             for b in range(CB):
                 nc.vector.tensor_tensor(xc[:, b, :], x_sb[b][:, tok], mean[:], ALU.subtract)
                 nc.gpsimd.tensor_tensor(sq[:, b, :], xc[:, b, :], xc[:, b, :], ALU.mult)
                 nc.tensor.matmul(
                     var[:], avg_bf16[:], sq[:, b, :], start=(b == 0), stop=(b == CB - 1)
                 )
-            rstd = norm.tile([P, T], F32, name="rstd")
+            rstd = norm.tile([P, w], F32, name="rstd")
             nc.scalar.activation(rstd[:], var[:], ACT.Abs_reciprocal_sqrt, bias=eps[:])
-            xhat = norm.tile([P, CB, T], F32, name="xhat")
+            xhat = norm.tile([P, CB, w], F32, name="xhat")
             for b in range(CB):
                 nc.vector.tensor_tensor(xhat[:, b, :], xc[:, b, :], rstd[:], ALU.mult)
-                nc.gpsimd.tensor_scalar(
+                nc.vector.tensor_scalar(
                     xn[:, b, tok], xhat[:, b, :], gain[:, b : b + 1], bias[:, b : b + 1],
                     ALU.mult, ALU.add,
                 )
 
         def hidden(t):
-            tok = slice(t * T, (t + 1) * T)
+            tok, w = chunk[t], WIDTHS[t]
             for hb in range(HB):
-                h = h_ps.tile([P, T], F32, name="h")
+                h = h_ps.tile([P, w], F32, name="h")
                 for b in range(CB):
                     nc.tensor.matmul(
                         h[:], wck_sb[:, b, hb * P : (hb + 1) * P], xn[:, b, tok],
                         start=(b == 0), stop=(b == CB - 1),
                     )
-                r = relu.tile([P, T], F32, name="r")
+                r = relu.tile([P, w], F32, name="r")
                 nc.scalar.activation(r[:], h[:], ACT.Relu)
                 nc.vector.tensor_tensor(hid[:, hb, tok], r[:], r[:], ALU.mult)
 
         def project(b, t):
-            tok = slice(t * T, (t + 1) * T)
-            y = y_ps.tile([P, T], F32, name="y")
+            tok, w = chunk[t], WIDTHS[t]
+            y = y_ps.tile([P, w], F32, name="y")
             for hb in range(HB):
                 nc.tensor.matmul(
                     y[:], wcv_sb[:, hb, b * P : (b + 1) * P], hid[:, hb, tok],
@@ -117,13 +119,13 @@ def tile_rwkv8_rosa_block_kernel(tc, base, x, ln_w, ln_b, wck, wcv, offs, out):
             )
             nc.sync.dma_start(out[b * P : (b + 1) * P, :], window[b][:])
 
-        layer_norm(0)
-        layer_norm(1)
-        for t in range(NT):
-            hidden(t)
-            if t + 2 < NT:
-                layer_norm(t + 2)
-            project(0, t)
+        for step in range(NT + 2):
+            if step < NT:
+                layer_norm(step)
+            if 1 <= step <= NT:
+                hidden(step - 1)
+            if step >= 2:
+                project(0, step - 2)
         place(0)
         for t in range(NT):
             project(1, t)

@@ -30,8 +30,7 @@ def tile_rwkv8_rosa_block_kernel(tc, base, x, ln_w, ln_b, wck, wcv, offs, out):
         tc.tile_pool(name="relu", bufs=6) as relu,
         tc.psum_pool(name="mean_ps", bufs=2) as mean_ps,
         tc.psum_pool(name="var_ps", bufs=1) as var_ps,
-        tc.psum_pool(name="h_ps", bufs=3) as h_ps,
-        tc.psum_pool(name="y_ps", bufs=2) as y_ps,
+        tc.psum_pool(name="prod_ps", bufs=5) as prod_ps,
     ):
         offsets = held.tile([P, N // 16], U16, name="offsets")
         x_sb = [held.tile([P, N], F32, name=f"x{b}") for b in range(CB)]
@@ -93,7 +92,7 @@ def tile_rwkv8_rosa_block_kernel(tc, base, x, ln_w, ln_b, wck, wcv, offs, out):
         def hidden(t):
             tok, w = chunk[t], WIDTHS[t]
             for hb in range(HB):
-                h = h_ps.tile([P, w], F32, name="h")
+                h = prod_ps.tile([P, w], F32, name="h", tag="prod")
                 for b in range(CB):
                     nc.tensor.matmul(
                         h[:], wck_sb[:, b, hb * P : (hb + 1) * P], xn[:, b, tok],
@@ -105,7 +104,7 @@ def tile_rwkv8_rosa_block_kernel(tc, base, x, ln_w, ln_b, wck, wcv, offs, out):
 
         def project(b, t):
             tok, w = chunk[t], WIDTHS[t]
-            y = y_ps.tile([P, w], F32, name="y")
+            y = prod_ps.tile([P, w], F32, name="y", tag="prod")
             for hb in range(HB):
                 nc.tensor.matmul(
                     y[:], wcv_sb[:, hb, b * P : (b + 1) * P], hid[:, hb, tok],

@@ -75,7 +75,7 @@ def tile_rwkv8_rosa_block_kernel(tc, base, x, ln_w, ln_b, wck, wcv, offs, out):
             var = var_ps.tile([P, w], F32, name="var")
             for b in range(CB):
                 nc.vector.tensor_tensor(xc[:, b, :], x_sb[b][:, tok], mean[:], ALU.subtract)
-                nc.gpsimd.tensor_tensor(sq[:, b, :], xc[:, b, :], xc[:, b, :], ALU.mult)
+                nc.scalar.activation(sq[:, b, :], xc[:, b, :], ACT.Square)
                 nc.tensor.matmul(
                     var[:], avg_bf16[:], sq[:, b, :], start=(b == 0), stop=(b == CB - 1)
                 )

@@ -63,6 +63,8 @@ def tile_rwkv8_rosa_block_kernel(tc, base, x, ln_w, ln_b, wck, wcv, offs, out):
         nc.vector.memset(avg_f32[:], 1.0 / C)
         nc.vector.memset(avg_bf16[:], 1.0 / C)
         nc.vector.memset(eps[:], EPS)
+        warm = held.tile([P, 1], F32, name="warm")
+        nc.scalar.activation(warm[:], eps[:], ACT.Abs_reciprocal_sqrt)
 
         def layer_norm(t):
             tok, w = chunk[t], WIDTHS[t]

@@ -86,10 +86,16 @@ def tile_rwkv8_rosa_block_kernel(tc, base, x, ln_w, ln_b, wck, wcv, offs, out):
             xhat = norm.tile([P, CB, w], F32, name="xhat")
             for b in range(CB):
                 nc.vector.tensor_tensor(xhat[:, b, :], xc[:, b, :], rstd[:], ALU.mult)
-                nc.vector.tensor_scalar(
-                    xn[:, b, tok], xhat[:, b, :], gain[:, b : b + 1], bias[:, b : b + 1],
-                    ALU.mult, ALU.add,
-                )
+                if w < T:
+                    nc.scalar.activation(
+                        xn[:, b, tok], xhat[:, b, :], ACT.Identity,
+                        bias=bias[:, b : b + 1], scale=gain[:, b : b + 1],
+                    )
+                else:
+                    nc.vector.tensor_scalar(
+                        xn[:, b, tok], xhat[:, b, :], gain[:, b : b + 1], bias[:, b : b + 1],
+                        ALU.mult, ALU.add,
+                    )
 
         def hidden(t):
             tok, w = chunk[t], WIDTHS[t]

@@ -51,6 +51,7 @@ def tile_rwkv8_rosa_block_kernel(tc, base, x, ln_w, ln_b, wck, wcv, offs, out):
         for t in range(NT):
             for b in range(CB):
                 nc.sync.dma_start(x_sb[b][:, chunk[t]], x[b * P : (b + 1) * P, chunk[t]])
+        nc.sync.dma_start(wcv_sb[:], wcv.rearrange("(b p) c -> p b c", p=P))
         nc.sync.dma_start(offsets[:], offs)
         for b in range(CB):
             nc.sync.dma_start(window[b][:], base[b * P : (b + 1) * P, :])
@@ -58,7 +59,6 @@ def tile_rwkv8_rosa_block_kernel(tc, base, x, ln_w, ln_b, wck, wcv, offs, out):
             nc.scalar.dma_start(gain[:], ln_w.rearrange("(b p) o -> p (b o)", p=P))
             nc.scalar.dma_start(bias[:], ln_b.rearrange("(b p) o -> p (b o)", p=P))
         nc.scalar.dma_start(wck_sb[:], wck.rearrange("(b p) h -> p b h", p=P))
-        nc.scalar.dma_start(wcv_sb[:], wcv.rearrange("(b p) c -> p b c", p=P))
 
         nc.vector.memset(avg_f32[:], 1.0 / C)
         nc.vector.memset(avg_bf16[:], 1.0 / C)

@@ -5,6 +5,7 @@ BF16 = mybir.dt.bfloat16
 U16 = mybir.dt.uint16
 ALU = mybir.AluOpType
 ACT = mybir.ActivationFunctionType
+AXIS = mybir.AxisListType
 
 P = 128
 C = 256
@@ -42,6 +43,8 @@ def tile_rwkv8_rosa_block_kernel(tc, base, x, ln_w, ln_b, wck, wcv, offs, out):
         wcv_sb = held.tile([P, HB, C], BF16, name="wcv_sb")
         gain = held.tile([P, CB], F32, name="gain")
         bias = held.tile([P, CB], F32, name="bias")
+        bias_parts = held.tile([P, CB, 2], BF16, name="bias_parts")
+        hid_bias = held.tile([P, HB], F32, name="hid_bias")
         eps = held.tile([P, 1], F32, name="eps")
         avg_f32 = held.tile([P, P], F32, name="avg_f32")
         avg_bf16 = held.tile([P, P], BF16, name="avg_bf16")
@@ -83,19 +86,23 @@ def tile_rwkv8_rosa_block_kernel(tc, base, x, ln_w, ln_b, wck, wcv, offs, out):
                 )
             rstd = norm.tile([P, w], F32, name="rstd")
             nc.scalar.activation(rstd[:], var[:], ACT.Abs_reciprocal_sqrt, bias=eps[:])
-            xhat = norm.tile([P, CB, w], F32, name="xhat")
             for b in range(CB):
-                nc.vector.tensor_tensor(xhat[:, b, :], xc[:, b, :], rstd[:], ALU.mult)
-                if w < T:
-                    nc.scalar.activation(
-                        xn[:, b, tok], xhat[:, b, :], ACT.Identity,
-                        bias=bias[:, b : b + 1], scale=gain[:, b : b + 1],
+                nc.vector.scalar_tensor_tensor(
+                    xn[:, b, tok], xc[:, b, :], gain[:, b : b + 1], rstd[:],
+                    ALU.mult, ALU.mult,
+                )
+
+        def project_bias():
+            nc.vector.tensor_copy(bias_parts[:, :, 0], bias[:])
+            nc.vector.tensor_tensor(bias_parts[:, :, 1], bias[:], bias_parts[:, :, 0], ALU.subtract)
+            parts = prod_ps.tile([P, HB, 2], F32, name="parts", tag="prod")
+            for hb in range(HB):
+                for b in range(CB):
+                    nc.tensor.matmul(
+                        parts[:, hb, :], wck_sb[:, b, hb * P : (hb + 1) * P], bias_parts[:, b, :],
+                        start=(b == 0), stop=(b == CB - 1),
                     )
-                else:
-                    nc.vector.tensor_scalar(
-                        xn[:, b, tok], xhat[:, b, :], gain[:, b : b + 1], bias[:, b : b + 1],
-                        ALU.mult, ALU.add,
-                    )
+            nc.vector.tensor_reduce(hid_bias[:], parts[:], AXIS.X, ALU.add)
 
         def hidden(t):
             tok, w = chunk[t], WIDTHS[t]
@@ -107,7 +114,7 @@ def tile_rwkv8_rosa_block_kernel(tc, base, x, ln_w, ln_b, wck, wcv, offs, out):
                         start=(b == 0), stop=(b == CB - 1),
                     )
                 r = relu.tile([P, w], F32, name="r")
-                nc.scalar.activation(r[:], h[:], ACT.Relu)
+                nc.scalar.activation(r[:], h[:], ACT.Relu, bias=hid_bias[:, hb : hb + 1])
                 nc.vector.tensor_tensor(hid[:, hb, tok], r[:], r[:], ALU.mult)
 
         def project(b, t):
@@ -129,6 +136,8 @@ def tile_rwkv8_rosa_block_kernel(tc, base, x, ln_w, ln_b, wck, wcv, offs, out):
         for step in range(NT + 2):
             if step < NT:
                 layer_norm(step)
+            if step == 0:
+                project_bias()
             if 1 <= step <= NT:
                 hidden(step - 1)
             if step >= 2:

@@ -37,19 +37,19 @@ def tile_rwkv8_rosa_block_kernel(tc, base, x, ln_w, ln_b, wck, wcv, offs, out):
         x_sb = [held.tile([P, N], F32, name=f"x{b}") for b in range(CB)]
         window = [held.tile([P, S], F32, name=f"window{b}") for b in range(CB)]
         y_sb = [held.tile([P, N], F32, name=f"y{b}") for b in range(CB)]
-        xn = held.tile([P, CB, N], BF16, name="xn")
+        xn = held.tile([P, CB, 2 + N], BF16, name="xn")
         hid = held.tile([P, HB, N], BF16, name="hid")
         wck_sb = held.tile([P, CB, H], BF16, name="wck_sb")
         wcv_sb = held.tile([P, HB, C], BF16, name="wcv_sb")
         gain = held.tile([P, CB], F32, name="gain")
         bias = held.tile([P, CB], F32, name="bias")
-        bias_parts = held.tile([P, CB, 2], BF16, name="bias_parts")
         hid_bias = held.tile([P, HB], F32, name="hid_bias")
         eps = held.tile([P, 1], F32, name="eps")
         avg_f32 = held.tile([P, P], F32, name="avg_f32")
         avg_bf16 = held.tile([P, P], BF16, name="avg_bf16")
 
         chunk = [slice(sum(WIDTHS[:t]), sum(WIDTHS[: t + 1])) for t in range(NT)]
+        chunk_xn = [slice(2 + tok.start, 2 + tok.stop) for tok in chunk]
 
         for t in range(NT):
             for b in range(CB):
@@ -74,52 +74,64 @@ def tile_rwkv8_rosa_block_kernel(tc, base, x, ln_w, ln_b, wck, wcv, offs, out):
             pair = norm.tile([P, w], F32, name="pair")
             nc.vector.tensor_tensor(pair[:], x_sb[0][:, tok], x_sb[1][:, tok], ALU.add)
             mean = mean_ps.tile([P, w], F32, name="mean")
-            nc.tensor.matmul(mean[:], avg_f32[:], pair[:], start=True, stop=True)
+            if t < NT - 2:
+                nc.tensor.matmul(mean[:], avg_f32[:], pair[:], start=True, stop=True)
+            else:
+                high = norm.tile([P, w], BF16, name="high")
+                low = norm.tile([P, w], BF16, name="low")
+                nc.scalar.copy(high[:], pair[:])
+                nc.vector.tensor_tensor(low[:], pair[:], high[:], ALU.subtract)
+                nc.tensor.matmul(mean[:], avg_bf16[:], high[:], start=True, stop=False)
+                nc.tensor.matmul(mean[:], avg_bf16[:], low[:], start=False, stop=True)
             xc = norm.tile([P, CB, w], F32, name="xc")
             sq = norm.tile([P, CB, w], BF16, name="sq")
             var = var_ps.tile([P, w], F32, name="var")
             for b in range(CB):
                 nc.vector.tensor_tensor(xc[:, b, :], x_sb[b][:, tok], mean[:], ALU.subtract)
                 nc.scalar.activation(sq[:, b, :], xc[:, b, :], ACT.Square)
-                nc.tensor.matmul(
-                    var[:], avg_bf16[:], sq[:, b, :], start=(b == 0), stop=(b == CB - 1)
-                )
+                if t < NT - 2:
+                    nc.tensor.matmul(
+                        var[:], avg_bf16[:], sq[:, b, :], start=(b == 0), stop=(b == CB - 1)
+                    )
+            if t >= NT - 2:
+                sq_pair = norm.tile([P, w], BF16, name="sq_pair")
+                nc.vector.tensor_tensor(sq_pair[:], sq[:, 0, :], sq[:, 1, :], ALU.add)
+                nc.tensor.matmul(var[:], avg_bf16[:], sq_pair[:], start=True, stop=True)
             rstd = norm.tile([P, w], F32, name="rstd")
             nc.scalar.activation(rstd[:], var[:], ACT.Abs_reciprocal_sqrt, bias=eps[:])
             for b in range(CB):
                 nc.vector.scalar_tensor_tensor(
-                    xn[:, b, tok], xc[:, b, :], gain[:, b : b + 1], rstd[:],
+                    xn[:, b, chunk_xn[t]], xc[:, b, :], gain[:, b : b + 1], rstd[:],
                     ALU.mult, ALU.mult,
                 )
 
-        def project_bias():
-            nc.vector.tensor_copy(bias_parts[:, :, 0], bias[:])
-            nc.vector.tensor_tensor(bias_parts[:, :, 1], bias[:], bias_parts[:, :, 0], ALU.subtract)
-            parts = prod_ps.tile([P, HB, 2], F32, name="parts", tag="prod")
-            for hb in range(HB):
-                for b in range(CB):
-                    nc.tensor.matmul(
-                        parts[:, hb, :], wck_sb[:, b, hb * P : (hb + 1) * P], bias_parts[:, b, :],
-                        start=(b == 0), stop=(b == CB - 1),
-                    )
-            nc.vector.tensor_reduce(hid_bias[:], parts[:], AXIS.X, ALU.add)
+        def bias_columns():
+            nc.vector.tensor_copy(xn[:, :, 0], bias[:])
+            nc.vector.tensor_tensor(xn[:, :, 1], bias[:], xn[:, :, 0], ALU.subtract)
 
         def hidden(t):
             tok, w = chunk[t], WIDTHS[t]
+            extra = 2 if t == 0 else 0
             for hb in range(HB):
-                h = prod_ps.tile([P, w], F32, name="h", tag="prod")
+                h = prod_ps.tile([P, extra + w], F32, name="h", tag="prod")
                 for b in range(CB):
                     nc.tensor.matmul(
-                        h[:], wck_sb[:, b, hb * P : (hb + 1) * P], xn[:, b, tok],
+                        h[:], wck_sb[:, b, hb * P : (hb + 1) * P],
+                        xn[:, b, chunk_xn[t].start - extra : chunk_xn[t].stop],
                         start=(b == 0), stop=(b == CB - 1),
                     )
+                if t == 0:
+                    nc.vector.tensor_reduce(
+                        hid_bias[:, hb : hb + 1], h[:, :extra], AXIS.X, ALU.add
+                    )
                 r = relu.tile([P, w], F32, name="r")
-                nc.scalar.activation(r[:], h[:], ACT.Relu, bias=hid_bias[:, hb : hb + 1])
+                nc.scalar.activation(
+                    r[:], h[:, extra:], ACT.Relu, bias=hid_bias[:, hb : hb + 1]
+                )
                 nc.vector.tensor_tensor(hid[:, hb, tok], r[:], r[:], ALU.mult)
 
-        def project(b, t):
-            tok, w = chunk[t], WIDTHS[t]
-            y = prod_ps.tile([P, w], F32, name="y", tag="prod")
+        def project(b, tok):
+            y = prod_ps.tile([P, tok.stop - tok.start], F32, name="y", tag="prod")
             for hb in range(HB):
                 nc.tensor.matmul(
                     y[:], wcv_sb[:, hb, b * P : (b + 1) * P], hid[:, hb, tok],
@@ -133,16 +145,18 @@ def tile_rwkv8_rosa_block_kernel(tc, base, x, ln_w, ln_b, wck, wcv, offs, out):
             )
             nc.sync.dma_start(out[b * P : (b + 1) * P, :], window[b][:])
 
-        for step in range(NT + 2):
+        for step in range(NT + 1):
             if step < NT:
                 layer_norm(step)
-            if step == 0:
-                project_bias()
+            if step == 1:
+                bias_columns()
             if 1 <= step <= NT:
                 hidden(step - 1)
-            if step >= 2:
-                project(0, step - 2)
+            if 2 <= step <= NT:
+                project(0, chunk[step - 2])
+        for half in (slice(N - T, N - T // 2), slice(N - T // 2, N)):
+            project(0, half)
         place(0)
-        for t in range(NT):
-            project(1, t)
+        for tok in chunk:
+            project(1, tok)
         place(1)

@@ -34,7 +34,7 @@ def tile_rwkv8_rosa_block_kernel(tc, base, x, ln_w, ln_b, wck, wcv, offs, out):
         tc.psum_pool(name="prod_ps", bufs=5) as prod_ps,
     ):
         offsets = held.tile([P, N // 16], U16, name="offsets")
-        x_sb = [held.tile([P, N], F32, name=f"x{b}") for b in range(CB)]
+        x_sb = held.tile([P, CB, N], F32, name="x_sb")
         window = [held.tile([P, S], F32, name=f"window{b}") for b in range(CB)]
         y_sb = [held.tile([P, N], F32, name=f"y{b}") for b in range(CB)]
         xn = held.tile([P, CB, 2 + N], BF16, name="xn")
@@ -51,9 +51,11 @@ def tile_rwkv8_rosa_block_kernel(tc, base, x, ln_w, ln_b, wck, wcv, offs, out):
         chunk = [slice(sum(WIDTHS[:t]), sum(WIDTHS[: t + 1])) for t in range(NT)]
         chunk_xn = [slice(2 + tok.start, 2 + tok.stop) for tok in chunk]
 
-        for t in range(NT):
-            for b in range(CB):
-                nc.sync.dma_start(x_sb[b][:, chunk[t]], x[b * P : (b + 1) * P, chunk[t]])
+        x_blocks = x.rearrange("(b p) t -> p b t", p=P)
+        for b in range(CB):
+            nc.sync.dma_start(x_sb[:, b, chunk[0]], x_blocks[:, b, chunk[0]])
+        for tok in chunk[1:]:
+            nc.sync.dma_start(x_sb[:, :, tok], x_blocks[:, :, tok])
         nc.sync.dma_start(wcv_sb[:], wcv.rearrange("(b p) c -> p b c", p=P))
         nc.sync.dma_start(offsets[:], offs)
         for b in range(CB):
@@ -69,10 +71,12 @@ def tile_rwkv8_rosa_block_kernel(tc, base, x, ln_w, ln_b, wck, wcv, offs, out):
         warm = held.tile([P, 1], F32, name="warm")
         nc.scalar.activation(warm[:], eps[:], ACT.Abs_reciprocal_sqrt)
 
-        def layer_norm(t):
+        means = {}
+
+        def take_mean(t):
             tok, w = chunk[t], WIDTHS[t]
             pair = norm.tile([P, w], F32, name="pair")
-            nc.vector.tensor_tensor(pair[:], x_sb[0][:, tok], x_sb[1][:, tok], ALU.add)
+            nc.vector.tensor_tensor(pair[:], x_sb[:, 0, tok], x_sb[:, 1, tok], ALU.add)
             mean = mean_ps.tile([P, w], F32, name="mean")
             if t < NT - 2:
                 nc.tensor.matmul(mean[:], avg_f32[:], pair[:], start=True, stop=True)
@@ -83,11 +87,15 @@ def tile_rwkv8_rosa_block_kernel(tc, base, x, ln_w, ln_b, wck, wcv, offs, out):
                 nc.vector.tensor_tensor(low[:], pair[:], high[:], ALU.subtract)
                 nc.tensor.matmul(mean[:], avg_bf16[:], high[:], start=True, stop=False)
                 nc.tensor.matmul(mean[:], avg_bf16[:], low[:], start=False, stop=True)
+            means[t] = mean
+
+        def layer_norm(t):
+            tok, w = chunk[t], WIDTHS[t]
             xc = norm.tile([P, CB, w], F32, name="xc")
             sq = norm.tile([P, CB, w], BF16, name="sq")
             var = var_ps.tile([P, w], F32, name="var")
             for b in range(CB):
-                nc.vector.tensor_tensor(xc[:, b, :], x_sb[b][:, tok], mean[:], ALU.subtract)
+                nc.vector.tensor_tensor(xc[:, b, :], x_sb[:, b, tok], means[t][:], ALU.subtract)
                 nc.scalar.activation(sq[:, b, :], xc[:, b, :], ACT.Square)
                 if t < NT - 2:
                     nc.tensor.matmul(
@@ -141,11 +149,14 @@ def tile_rwkv8_rosa_block_kernel(tc, base, x, ln_w, ln_b, wck, wcv, offs, out):
 
         def place(b):
             nc.vector.tensor_tensor(
-                window[b][:].indirect(offsets[:]), x_sb[b][:], y_sb[b][:], ALU.add
+                window[b][:].indirect(offsets[:]), x_sb[:, b, :], y_sb[b][:], ALU.add
             )
             nc.sync.dma_start(out[b * P : (b + 1) * P, :], window[b][:])
 
+        take_mean(0)
         for step in range(NT + 1):
+            if step + 1 < NT:
+                take_mean(step + 1)
             if step < NT:
                 layer_norm(step)
             if step == 1:

import concourse.mybir as mybir

F32 = mybir.dt.float32
BF16 = mybir.dt.bfloat16
U16 = mybir.dt.uint16
ALU = mybir.AluOpType
ACT = mybir.ActivationFunctionType
AXIS = mybir.AxisListType

P = 128
C = 256
H = 1024
S = 4096
N = 2048
CB = C // P
HB = H // P
T = 512
WIDTHS = (T // 2, T // 2, T, T, T)
NT = len(WIDTHS)
assert sum(WIDTHS) == N
EPS = 1e-5

FLOPS = 2 * 2 * C * H * N


def tile_rwkv8_rosa_block_kernel(tc, base, x, ln_w, ln_b, wck, wcv, offs, out):
    nc = tc.nc
    with (
        tc.tile_pool(name="held", bufs=1) as held,
        tc.tile_pool(name="norm", bufs=3) as norm,
        tc.tile_pool(name="relu", bufs=6) as relu,
        tc.psum_pool(name="mean_ps", bufs=2) as mean_ps,
        tc.psum_pool(name="var_ps", bufs=1) as var_ps,
        tc.psum_pool(name="prod_ps", bufs=5) as prod_ps,
    ):
        offsets = held.tile([P, N // 16], U16, name="offsets")
        x_sb = held.tile([P, CB, N], F32, name="x_sb")
        window = [held.tile([P, S], F32, name=f"window{b}") for b in range(CB)]
        y_sb = [held.tile([P, N], F32, name=f"y{b}") for b in range(CB)]
        xn = held.tile([P, CB, 2 + N], BF16, name="xn")
        hid = held.tile([P, HB, N], BF16, name="hid")
        wck_sb = held.tile([P, CB, H], BF16, name="wck_sb")
        wcv_sb = held.tile([P, HB, C], BF16, name="wcv_sb")
        gain = held.tile([P, CB], F32, name="gain")
        bias = held.tile([P, CB], F32, name="bias")
        hid_bias = held.tile([P, HB], F32, name="hid_bias")
        eps = held.tile([P, 1], F32, name="eps")
        avg_f32 = held.tile([P, P], F32, name="avg_f32")
        avg_bf16 = held.tile([P, P], BF16, name="avg_bf16")

        chunk = [slice(sum(WIDTHS[:t]), sum(WIDTHS[: t + 1])) for t in range(NT)]
        chunk_xn = [slice(2 + tok.start, 2 + tok.stop) for tok in chunk]

        x_blocks = x.rearrange("(b p) t -> p b t", p=P)
        for b in range(CB):
            nc.sync.dma_start(x_sb[:, b, chunk[0]], x_blocks[:, b, chunk[0]])
        for tok in chunk[1:]:
            nc.sync.dma_start(x_sb[:, :, tok], x_blocks[:, :, tok])
        nc.sync.dma_start(wcv_sb[:], wcv.rearrange("(b p) c -> p b c", p=P))
        nc.sync.dma_start(offsets[:], offs)
        for b in range(CB):
            nc.sync.dma_start(window[b][:], base[b * P : (b + 1) * P, :])
        with nc.allow_non_contiguous_dma(reason="one gain and one bias to a partition"):
            nc.scalar.dma_start(gain[:], ln_w.rearrange("(b p) o -> p (b o)", p=P))
            nc.scalar.dma_start(bias[:], ln_b.rearrange("(b p) o -> p (b o)", p=P))
        nc.scalar.dma_start(wck_sb[:], wck.rearrange("(b p) h -> p b h", p=P))

        nc.vector.memset(avg_f32[:], 1.0 / C)
        nc.vector.memset(avg_bf16[:], 1.0 / C)
        nc.vector.memset(eps[:], EPS)
        warm = held.tile([P, 1], F32, name="warm")
        nc.scalar.activation(warm[:], eps[:], ACT.Abs_reciprocal_sqrt)

        means = {}

        def take_mean(t):
            tok, w = chunk[t], WIDTHS[t]
            pair = norm.tile([P, w], F32, name="pair")
            nc.vector.tensor_tensor(pair[:], x_sb[:, 0, tok], x_sb[:, 1, tok], ALU.add)
            mean = mean_ps.tile([P, w], F32, name="mean")
            if t < NT - 2:
                nc.tensor.matmul(mean[:], avg_f32[:], pair[:], start=True, stop=True)
            else:
                high = norm.tile([P, w], BF16, name="high")
                low = norm.tile([P, w], BF16, name="low")
                nc.scalar.copy(high[:], pair[:])
                nc.vector.tensor_tensor(low[:], pair[:], high[:], ALU.subtract)
                nc.tensor.matmul(mean[:], avg_bf16[:], high[:], start=True, stop=False)
                nc.tensor.matmul(mean[:], avg_bf16[:], low[:], start=False, stop=True)
            means[t] = mean

        def layer_norm(t):
            tok, w = chunk[t], WIDTHS[t]
            xc = norm.tile([P, CB, w], F32, name="xc")
            sq = norm.tile([P, CB, w], BF16, name="sq")
            var = var_ps.tile([P, w], F32, name="var")
            for b in range(CB):
                nc.vector.tensor_tensor(xc[:, b, :], x_sb[:, b, tok], means[t][:], ALU.subtract)
                nc.scalar.activation(sq[:, b, :], xc[:, b, :], ACT.Square)
                if t < NT - 2:
                    nc.tensor.matmul(
                        var[:], avg_bf16[:], sq[:, b, :], start=(b == 0), stop=(b == CB - 1)
                    )
            if t >= NT - 2:
                sq_pair = norm.tile([P, w], BF16, name="sq_pair")
                nc.vector.tensor_tensor(sq_pair[:], sq[:, 0, :], sq[:, 1, :], ALU.add)
                nc.tensor.matmul(var[:], avg_bf16[:], sq_pair[:], start=True, stop=True)
            rstd = norm.tile([P, w], F32, name="rstd")
            nc.scalar.activation(rstd[:], var[:], ACT.Abs_reciprocal_sqrt, bias=eps[:])
            for b in range(CB):
                nc.vector.scalar_tensor_tensor(
                    xn[:, b, chunk_xn[t]], xc[:, b, :], gain[:, b : b + 1], rstd[:],
                    ALU.mult, ALU.mult,
                )

        def bias_columns():
            nc.vector.tensor_copy(xn[:, :, 0], bias[:])
            nc.vector.tensor_tensor(xn[:, :, 1], bias[:], xn[:, :, 0], ALU.subtract)

        def hidden(t):
            tok, w = chunk[t], WIDTHS[t]
            extra = 2 if t == 0 else 0
            for hb in range(HB):
                h = prod_ps.tile([P, extra + w], F32, name="h", tag="prod")
                for b in range(CB):
                    nc.tensor.matmul(
                        h[:], wck_sb[:, b, hb * P : (hb + 1) * P],
                        xn[:, b, chunk_xn[t].start - extra : chunk_xn[t].stop],
                        start=(b == 0), stop=(b == CB - 1),
                    )
                if t == 0:
                    nc.vector.tensor_reduce(
                        hid_bias[:, hb : hb + 1], h[:, :extra], AXIS.X, ALU.add
                    )
                r = relu.tile([P, w], F32, name="r")
                nc.scalar.activation(
                    r[:], h[:, extra:], ACT.Relu, bias=hid_bias[:, hb : hb + 1]
                )
                nc.vector.tensor_tensor(hid[:, hb, tok], r[:], r[:], ALU.mult)

        def project(b, tok):
            y = prod_ps.tile([P, tok.stop - tok.start], F32, name="y", tag="prod")
            for hb in range(HB):
                nc.tensor.matmul(
                    y[:], wcv_sb[:, hb, b * P : (b + 1) * P], hid[:, hb, tok],
                    start=(hb == 0), stop=(hb == HB - 1),
                )
            nc.scalar.copy(y_sb[b][:, tok], y[:])

        def place(b):
            nc.vector.tensor_tensor(
                window[b][:].indirect(offsets[:]), x_sb[:, b, :], y_sb[b][:], ALU.add
            )
            nc.sync.dma_start(out[b * P : (b + 1) * P, :], window[b][:])

        take_mean(0)
        for step in range(NT + 1):
            if step + 1 < NT:
                take_mean(step + 1)
            if step < NT:
                layer_norm(step)
            if step == 1:
                bias_columns()
            if 1 <= step <= NT:
                hidden(step - 1)
            if 2 <= step <= NT:
                project(0, chunk[step - 2])
        for half in (slice(N - T, N - T // 2), slice(N - T // 2, N)):
            project(0, half)
        place(0)
        for tok in chunk:
            project(1, tok)
        place(1)
